import numpy as np
import ml_dtypes


def mxq(x, axis, fmt="e4m3"):
    dtype, down = {"e4m3": (ml_dtypes.float8_e4m3fn, 7), "e5m2": (ml_dtypes.float8_e5m2, 14)}[fmt]
    v = np.moveaxis(np.asarray(x, np.float32).astype(ml_dtypes.bfloat16).astype(np.float64), axis, -1)
    blocks = v.reshape(v.shape[:-1] + (-1, 32))
    amax = np.abs(blocks).max(-1, keepdims=True)
    byte = np.maximum(np.where(amax > 0, np.frexp(amax)[1] - 1 + 127, 0) - down, 1)
    scale = np.exp2(byte - 127.0)
    codes = (blocks / scale).astype(np.float32).astype(dtype).astype(np.float64)
    return np.moveaxis((codes * scale).reshape(v.shape), -1, axis)


WIDE = False


def mx_kscale(k):
    if not WIDE:
        return np.ones(k)
    levels = np.array([10, -10, 5, -5, 0])
    a = np.random.permutation(np.resize(levels, k // 512 * 4)).reshape(k // 512, 4)
    idx = np.arange(k)
    return np.exp2(a[idx // 512, idx % 128 // 32])


BF16 = ml_dtypes.bfloat16


def bf(x):
    return np.asarray(x, np.float32).astype(BF16)


def f64(x):
    return np.asarray(x).astype(np.float64)


E2M1 = np.array([0.0, 0.5, 1.0, 1.5, 2.0, 3.0, 4.0, 6.0, -0.0, -0.5, -1.0, -1.5, -2.0, -3.0, -4.0, -6.0])


def pack_weight(w, fmt):
    k, n = w.shape
    w = f64(bf(w)).reshape(k // 32, 32, n)
    amax = np.abs(w).max(1)
    if fmt == "e4m3":
        byte = np.frexp(amax)[1] - 1 + 127 - 7
    else:
        mant, ex = np.frexp(amax / 6.0)
        byte = np.where(mant > 0.5, ex, ex - 1) + 127
    byte = np.clip(np.where(amax > 0, byte, 1), 1, 254)
    scaled = (w * np.exp2(127.0 - byte)[:, None, :]).reshape(k, n).astype(np.float32)
    by_word = np.ascontiguousarray(scaled.reshape(k // 512, 128, 4, n).transpose(0, 1, 3, 2))
    if fmt == "e4m3":
        words = by_word.astype(ml_dtypes.float8_e4m3fn).view(np.uint8)
    else:
        c = by_word.astype(ml_dtypes.float4_e2m1fn).view(np.uint8) & 0xF
        words = c[..., 0::2] | (c[..., 1::2] << 4)
    return np.ascontiguousarray(words), np.ascontiguousarray(byte.astype(np.uint8).reshape(k // 512, 16, n))


def unpack_weight(words, scales, fmt):
    g, p, n, _ = words.shape
    if fmt == "e4m3":
        vals = np.ascontiguousarray(words).view(ml_dtypes.float8_e4m3fn).astype(np.float64)
    else:
        nib = np.empty((g, p, n, 4), np.uint8)
        nib[..., 0::2] = words & 0xF
        nib[..., 1::2] = words >> 4
        vals = E2M1[nib]
    vals = vals * np.repeat(np.exp2(scales.astype(np.float64) - 127.0), 8, axis=1)[..., None]
    return vals.transpose(0, 1, 3, 2).reshape(g * 512, n)


M, N, K = 256, 4096, 2048


def setup_inputs():
    s = mx_kscale(K)
    w = np.random.standard_normal((K, N)) * 0.022 / s[:, None]
    b_words, b_scales = pack_weight(w, "e4m3")
    return {"a": bf(np.random.standard_normal((M, K)) * s), "b_words": b_words, "b_scales": b_scales,
            "bias": bf(np.random.standard_normal(N))}


def reference(a, b_words, b_scales, bias):
    w = unpack_weight(b_words, b_scales, "e4m3")
    return (mxq(f64(a), 1, "e4m3") @ w) + f64(bias)[None, :]

@@ -1,0 +1,158 @@
+from contextlib import ExitStack
+
+import concourse.masks as masks
+import concourse.mybir as mybir
+
+F32 = mybir.dt.float32
+BF16 = mybir.dt.bfloat16
+I32 = mybir.dt.int32
+U32 = mybir.dt.uint32
+U8 = mybir.dt.uint8
+FP8X4 = mybir.dt.float8_e4m3fn_x4
+
+M, K, N = 256, 2048, 4096
+FLOPS = 2 * M * K * N
+
+P = 128
+GROUPS = K // 512
+ROWS = M // P
+BANK = 512
+CHUNKS = ((0, 2048), (2048, 1024), (3072, 1024))
+
+
+def tile_ac4kdotscaleop_kernel(tc, a, b_words, b_scales, bias, out):
+    nc = tc.nc
+    with ExitStack() as ctx:
+        ctx.enter_context(tc.manual_schedule())
+        keep = ctx.enter_context(tc.tile_pool(name="keep", bufs=1))
+        psum = ctx.enter_context(tc.psum_pool(name="psum", bufs=8))
+
+        planes = keep.tile([P, N], U8, align_bytes=64)
+        bias_rows = keep.tile([P, BANK], BF16)
+        a_sb = keep.tile([P, ROWS * K], BF16)
+        grouped = keep.tile([P, GROUPS, ROWS * P * 4], BF16, align_bytes=64)
+        a_codes = keep.tile([P, GROUPS, ROWS * P], U32, align_bytes=64)
+        a_scales = keep.tile([P, GROUPS, ROWS * P], U8, align_bytes=64)
+        bias_bc = keep.tile([P, N], F32)
+        ident_bf = keep.tile([P, P], BF16)
+        ident = keep.tile([P, P], F32)
+
+        nc.vector.memset(bias_rows[:], 0.0)
+        nc.vector.memset(planes[:].bitcast(I32), 0)
+
+        nc.sync.dma_start(out=a_sb[:], in_=a.rearrange("(p j) k -> p (j k)", j=ROWS))
+        nc.scalar.dma_start(
+            out=bias_rows[0 : N // BANK, :], in_=bias.rearrange("(r n) -> r n", n=BANK)
+        )
+        scale_words = b_scales.bitcast(I32)
+        for q in range(4):
+            nc.sync.dma_start(
+                out=planes[32 * q : 32 * q + 16, :].bitcast(I32),
+                in_=scale_words[:, 4 * q : 4 * q + 4, :],
+            )
+        w_sb = []
+        for c, (n0, width) in enumerate(CHUNKS):
+            per_group = []
+            for g in range(GROUPS):
+                w_tile = keep.tile([P, width], U32, align_bytes=64, name="w%d_%d" % (c, g))
+                nc.sync.dma_start(
+                    out=w_tile[:].bitcast(I32),
+                    in_=b_words[g]
+                    .rearrange("p n t -> p (n t)")[:, 4 * n0 : 4 * (n0 + width)]
+                    .bitcast(I32),
+                )
+                per_group.append(w_tile)
+            w_sb.append(per_group)
+
+        masks.make_identity(nc, ident_bf[:])
+        masks.make_identity(nc, ident[:])
+
+        def spread_bias(r, engine_copy):
+            bank = psum.tile([P, BANK], F32, tag="bank", name="bias_ps%d" % r)
+            nc.tensor.matmul(
+                out=bank[:],
+                lhsT=ident_bf[:, r : r + 1].to_broadcast([P, P]),
+                rhs=bias_rows[:],
+                start=True,
+                stop=True,
+            )
+            engine_copy(out=bias_bc[:, r * BANK : (r + 1) * BANK], in_=bank[:])
+
+        spread_bias(0, nc.scalar.copy)
+        spread_bias(1, nc.vector.tensor_copy)
+        spread_bias(2, nc.scalar.copy)
+        spread_bias(3, nc.vector.tensor_copy)
+
+        a_words = a_sb[:].bitcast(F32)
+        half = K // 2
+        banks = []
+        for g in range(GROUPS):
+            xt = psum.tile([P, ROWS, 2, P], F32, tag="bank", name="xt%d" % g)
+            for j in range(ROWS):
+                for u in range(2):
+                    nc.tensor.transpose(
+                        xt[:, j, u, :],
+                        a_words[:, j * half + 256 * g + u : j * half + 256 * (g + 1) : 2],
+                        ident[:],
+                    )
+            banks.append(xt)
+
+        def regroup(g, engine_copy):
+            engine_copy(
+                out=grouped[:, g, :].bitcast(F32).rearrange("p (j m u) -> p j m u", j=ROWS, u=2),
+                in_=banks[g][:].rearrange("p j u m -> p j m u"),
+            )
+
+        def quantise(g):
+            nc.vector.quantize_mx(
+                out=a_codes[:, g, :].bitcast(FP8X4),
+                scales=a_scales[:, g, :],
+                in_=grouped[:, g, :],
+            )
+
+        regroup(0, nc.vector.tensor_copy)
+        regroup(1, nc.scalar.copy)
+        quantise(0)
+        regroup(2, nc.vector.tensor_copy)
+        regroup(3, nc.scalar.copy)
+        quantise(1)
+        quantise(2)
+        quantise(3)
+
+        spread_bias(4, nc.scalar.copy)
+        spread_bias(5, nc.scalar.copy)
+        spread_bias(6, nc.vector.tensor_copy)
+        spread_bias(7, nc.vector.tensor_copy)
+
+        out_rows = out.rearrange("(p j) n -> p j n", j=ROWS)
+        for c, (n0, width) in enumerate(CHUNKS):
+            tiles = width // BANK
+            acc = [
+                [
+                    psum.tile([P, BANK], F32, tag="bank", name="acc%d_%d_%d" % (c, j, t))
+                    for t in range(tiles)
+                ]
+                for j in range(ROWS)
+            ]
+            for g in range(GROUPS):
+                for j in range(ROWS):
+                    for t in range(tiles):
+                        nc.tensor.matmul_mx(
+                            out=acc[j][t][:],
+                            lhsT=a_codes[:, g, j * P : (j + 1) * P].bitcast(FP8X4),
+                            lhsT_scale=a_scales[:, g, j * P : (j + 1) * P],
+                            rhs=w_sb[c][g][:, t * BANK : (t + 1) * BANK].bitcast(FP8X4),
+                            rhs_scale=planes[4 * g : P, n0 + t * BANK : n0 + (t + 1) * BANK],
+                            start=(g == 0),
+                            stop=(g == GROUPS - 1),
+                        )
+            o_sb = keep.tile([P, ROWS, width], F32, name="o%d" % c)
+            for j in range(ROWS):
+                for t in range(tiles):
+                    nc.vector.tensor_tensor(
+                        out=o_sb[:, j, t * BANK : (t + 1) * BANK],
+                        in0=acc[j][t][:],
+                        in1=bias_bc[:, n0 + t * BANK : n0 + (t + 1) * BANK],
+                        op=mybir.AluOpType.add,
+                    )
+            nc.sync.dma_start(out=out_rows[:, :, n0 : n0 + width], in_=o_sb[:])

@@ -15,9 +15,10 @@ FLOPS = 2 * M * K * N
 
 P = 128
 GROUPS = K // 512
-ROWS = M // P
+ROW_TILES = M // P
 BANK = 512
 CHUNKS = ((0, 2048), (2048, 1024), (3072, 1024))
+WARM = 5
 
 
 def tile_ac4kdotscaleop_kernel(tc, a, b_words, b_scales, bias, out):
@@ -29,21 +30,27 @@ def tile_ac4kdotscaleop_kernel(tc, a, b_words, b_scales, bias, out):
 
         planes = keep.tile([P, N], U8, align_bytes=64)
         bias_rows = keep.tile([P, BANK], BF16)
-        a_sb = keep.tile([P, ROWS * K], BF16)
-        grouped = keep.tile([P, GROUPS, ROWS * P * 4], BF16, align_bytes=64)
-        a_codes = keep.tile([P, GROUPS, ROWS * P], U32, align_bytes=64)
-        a_scales = keep.tile([P, GROUPS, ROWS * P], U8, align_bytes=64)
+        warm = keep.tile([P, BANK], BF16)
+        grouped = keep.tile([P, ROW_TILES, GROUPS, P * 4], BF16, align_bytes=64)
+        a_codes = keep.tile([P, ROW_TILES, GROUPS, P], U32, align_bytes=64)
+        a_scales = keep.tile([P, ROW_TILES, GROUPS, P], U8, align_bytes=64)
         bias_bc = keep.tile([P, N], F32)
-        ident_bf = keep.tile([P, P], BF16)
         ident = keep.tile([P, P], F32)
 
         nc.vector.memset(bias_rows[:], 0.0)
+        nc.vector.memset(warm[:], 0.0)
         nc.vector.memset(planes[:].bitcast(I32), 0)
 
-        nc.sync.dma_start(out=a_sb[:], in_=a.rearrange("(p j) k -> p (j k)", j=ROWS))
-        nc.scalar.dma_start(
-            out=bias_rows[0 : N // BANK, :], in_=bias.rearrange("(r n) -> r n", n=BANK)
-        )
+        a_tiles = a.rearrange("(j p) k -> j p k", p=P)
+        a_sb = []
+        for j in range(ROW_TILES):
+            a_j = keep.tile([P, K], BF16, name="a%d" % j)
+            nc.sync.dma_start(out=a_j[:], in_=a_tiles[j])
+            a_sb.append(a_j)
+            if j == 0:
+                nc.sync.dma_start(
+                    out=bias_rows[0 : N // BANK, :], in_=bias.rearrange("(r n) -> r n", n=BANK)
+                )
         scale_words = b_scales.bitcast(I32)
         for q in range(4):
             nc.sync.dma_start(
@@ -64,67 +71,80 @@ def tile_ac4kdotscaleop_kernel(tc, a, b_words, b_scales, bias, out):
                 per_group.append(w_tile)
             w_sb.append(per_group)
 
-        masks.make_identity(nc, ident_bf[:])
         masks.make_identity(nc, ident[:])
 
-        def spread_bias(r, engine_copy):
+        warm_ps = psum.tile([P, BANK], F32, tag="bank")
+        for i in range(WARM):
+            nc.tensor.matmul(out=warm_ps[:], lhsT=warm[:, 0:P], rhs=warm[:], start=True, stop=True)
+
+        selector = ident[:].bitcast(BF16)
+
+        def spread_bias(r):
             bank = psum.tile([P, BANK], F32, tag="bank", name="bias_ps%d" % r)
             nc.tensor.matmul(
                 out=bank[:],
-                lhsT=ident_bf[:, r : r + 1].to_broadcast([P, P]),
+                lhsT=selector[:, 2 * r + 1 : 2 * r + 2].to_broadcast([P, P]),
                 rhs=bias_rows[:],
                 start=True,
                 stop=True,
             )
+            return bank
+
+        def keep_bias(r, bank, engine_copy):
             engine_copy(out=bias_bc[:, r * BANK : (r + 1) * BANK], in_=bank[:])
 
-        spread_bias(0, nc.scalar.copy)
-        spread_bias(1, nc.vector.tensor_copy)
-        spread_bias(2, nc.scalar.copy)
-        spread_bias(3, nc.vector.tensor_copy)
-
-        a_words = a_sb[:].bitcast(F32)
-        half = K // 2
-        banks = []
-        for g in range(GROUPS):
-            xt = psum.tile([P, ROWS, 2, P], F32, tag="bank", name="xt%d" % g)
-            for j in range(ROWS):
+        def transpose_pair(j, pair):
+            a_words = a_sb[j][:].bitcast(F32)
+            xt = psum.tile([P, 2, 2, P], F32, tag="bank", name="xt%d_%d" % (j, pair))
+            for h in range(2):
+                g = 2 * pair + h
                 for u in range(2):
                     nc.tensor.transpose(
-                        xt[:, j, u, :],
-                        a_words[:, j * half + 256 * g + u : j * half + 256 * (g + 1) : 2],
-                        ident[:],
+                        xt[:, h, u, :], a_words[:, 256 * g + u : 256 * (g + 1) : 2], ident[:]
                     )
-            banks.append(xt)
+            return xt
 
-        def regroup(g, engine_copy):
+        def regroup(j, pair, xt, engine_copy):
             engine_copy(
-                out=grouped[:, g, :].bitcast(F32).rearrange("p (j m u) -> p j m u", j=ROWS, u=2),
-                in_=banks[g][:].rearrange("p j u m -> p j m u"),
+                out=grouped[:, j, 2 * pair : 2 * pair + 2, :]
+                .bitcast(F32)
+                .rearrange("p h (m u) -> p h m u", u=2),
+                in_=xt[:].rearrange("p h u m -> p h m u"),
             )
 
-        def quantise(g):
+        def quantise(j, pair):
             nc.vector.quantize_mx(
-                out=a_codes[:, g, :].bitcast(FP8X4),
-                scales=a_scales[:, g, :],
-                in_=grouped[:, g, :],
+                out=a_codes[:, j, 2 * pair : 2 * pair + 2, :]
+                .rearrange("p h m -> p (h m)")
+                .bitcast(FP8X4),
+                scales=a_scales[:, j, 2 * pair : 2 * pair + 2, :].rearrange("p h m -> p (h m)"),
+                in_=grouped[:, j, 2 * pair : 2 * pair + 2, :].rearrange("p h c -> p (h c)"),
             )
 
-        regroup(0, nc.vector.tensor_copy)
-        regroup(1, nc.scalar.copy)
-        quantise(0)
-        regroup(2, nc.vector.tensor_copy)
-        regroup(3, nc.scalar.copy)
-        quantise(1)
-        quantise(2)
-        quantise(3)
+        xt00 = transpose_pair(0, 0)
+        xt01 = transpose_pair(0, 1)
+        regroup(0, 0, xt00, nc.vector.tensor_copy)
+        regroup(0, 1, xt01, nc.scalar.copy)
+        quantise(0, 0)
+        quantise(0, 1)
+        first = [spread_bias(r) for r in range(4)]
+        keep_bias(0, first[0], nc.scalar.copy)
+        keep_bias(1, first[1], nc.vector.tensor_copy)
+        keep_bias(2, first[2], nc.scalar.copy)
+        keep_bias(3, first[3], nc.vector.tensor_copy)
+        xt10 = transpose_pair(1, 0)
+        xt11 = transpose_pair(1, 1)
+        regroup(1, 0, xt10, nc.vector.tensor_copy)
+        regroup(1, 1, xt11, nc.scalar.copy)
+        quantise(1, 0)
+        quantise(1, 1)
+        second = [spread_bias(r) for r in range(4, 8)]
+        keep_bias(4, second[0], nc.scalar.copy)
+        keep_bias(5, second[1], nc.scalar.copy)
+        keep_bias(6, second[2], nc.vector.tensor_copy)
+        keep_bias(7, second[3], nc.vector.tensor_copy)
 
-        spread_bias(4, nc.scalar.copy)
-        spread_bias(5, nc.scalar.copy)
-        spread_bias(6, nc.vector.tensor_copy)
-        spread_bias(7, nc.vector.tensor_copy)
-
-        out_rows = out.rearrange("(p j) n -> p j n", j=ROWS)
+        out_tiles = out.rearrange("(j p) n -> j p n", p=P)
         for c, (n0, width) in enumerate(CHUNKS):
             tiles = width // BANK
             acc = [
@@ -132,27 +152,27 @@ def tile_ac4kdotscaleop_kernel(tc, a, b_words, b_scales, bias, out):
                     psum.tile([P, BANK], F32, tag="bank", name="acc%d_%d_%d" % (c, j, t))
                     for t in range(tiles)
                 ]
-                for j in range(ROWS)
+                for j in range(ROW_TILES)
             ]
             for g in range(GROUPS):
-                for j in range(ROWS):
+                for j in range(ROW_TILES):
                     for t in range(tiles):
                         nc.tensor.matmul_mx(
                             out=acc[j][t][:],
-                            lhsT=a_codes[:, g, j * P : (j + 1) * P].bitcast(FP8X4),
-                            lhsT_scale=a_scales[:, g, j * P : (j + 1) * P],
+                            lhsT=a_codes[:, j, g, :].bitcast(FP8X4),
+                            lhsT_scale=a_scales[:, j, g, :],
                             rhs=w_sb[c][g][:, t * BANK : (t + 1) * BANK].bitcast(FP8X4),
                             rhs_scale=planes[4 * g : P, n0 + t * BANK : n0 + (t + 1) * BANK],
                             start=(g == 0),
                             stop=(g == GROUPS - 1),
                         )
-            o_sb = keep.tile([P, ROWS, width], F32, name="o%d" % c)
-            for j in range(ROWS):
+            for j in range(ROW_TILES):
+                o_sb = keep.tile([P, width], F32, name="o%d_%d" % (c, j))
                 for t in range(tiles):
                     nc.vector.tensor_tensor(
-                        out=o_sb[:, j, t * BANK : (t + 1) * BANK],
+                        out=o_sb[:, t * BANK : (t + 1) * BANK],
                         in0=acc[j][t][:],
                         in1=bias_bc[:, n0 + t * BANK : n0 + (t + 1) * BANK],
                         op=mybir.AluOpType.add,
                     )
-            nc.sync.dma_start(out=out_rows[:, :, n0 : n0 + width], in_=o_sb[:])
+                nc.sync.dma_start(out=out_tiles[j][:, n0 : n0 + width], in_=o_sb[:])

@@ -51,12 +51,6 @@ def tile_ac4kdotscaleop_kernel(tc, a, b_words, b_scales, bias, out):
                 nc.sync.dma_start(
                     out=bias_rows[0 : N // BANK, :], in_=bias.rearrange("(r n) -> r n", n=BANK)
                 )
-        scale_words = b_scales.bitcast(I32)
-        for q in range(4):
-            nc.sync.dma_start(
-                out=planes[32 * q : 32 * q + 16, :].bitcast(I32),
-                in_=scale_words[:, 4 * q : 4 * q + 4, :],
-            )
         w_sb = []
         for c, (n0, width) in enumerate(CHUNKS):
             per_group = []
@@ -72,6 +66,12 @@ def tile_ac4kdotscaleop_kernel(tc, a, b_words, b_scales, bias, out):
             w_sb.append(per_group)
 
         masks.make_identity(nc, ident[:])
+        scale_words = b_scales.bitcast(F32)
+        for q in range(4):
+            nc.gpsimd.dma_start(
+                out=planes[32 * q : 32 * q + 16, :].bitcast(F32),
+                in_=scale_words[:, 4 * q : 4 * q + 4, :],
+            )
 
         warm_ps = psum.tile([P, BANK], F32, tag="bank")
         for i in range(WARM):

@@ -28,7 +28,7 @@ def tile_ac4kdotscaleop_kernel(tc, a, b_words, b_scales, bias, out):
         keep = ctx.enter_context(tc.tile_pool(name="keep", bufs=1))
         psum = ctx.enter_context(tc.psum_pool(name="psum", bufs=8))
 
-        planes = keep.tile([P, N], U8, align_bytes=64)
+        planes = [keep.tile([P, N // 2], U8, align_bytes=64, name="planes%d" % h) for h in range(2)]
         bias_rows = keep.tile([P, BANK], BF16)
         warm = keep.tile([P, BANK], BF16)
         grouped = keep.tile([P, ROW_TILES, GROUPS, P * 4], BF16, align_bytes=64)
@@ -39,7 +39,8 @@ def tile_ac4kdotscaleop_kernel(tc, a, b_words, b_scales, bias, out):
 
         nc.vector.memset(bias_rows[:], 0.0)
         nc.vector.memset(warm[:], 0.0)
-        nc.vector.memset(planes[:].bitcast(I32), 0)
+        nc.vector.memset(planes[0][:].bitcast(I32), 0)
+        nc.vector.memset(planes[1][:].bitcast(I32), 0)
 
         a_tiles = a.rearrange("(j p) k -> j p k", p=P)
         a_sb = []
@@ -51,6 +52,12 @@ def tile_ac4kdotscaleop_kernel(tc, a, b_words, b_scales, bias, out):
                 nc.sync.dma_start(
                     out=bias_rows[0 : N // BANK, :], in_=bias.rearrange("(r n) -> r n", n=BANK)
                 )
+        scale_words = b_scales.bitcast(I32)
+        for q in range(4):
+            nc.sync.dma_start(
+                out=planes[0][32 * q : 32 * q + 16, :].bitcast(I32),
+                in_=scale_words[:, 4 * q : 4 * q + 4, 0 : N // 8],
+            )
         w_sb = []
         for c, (n0, width) in enumerate(CHUNKS):
             per_group = []
@@ -66,11 +73,11 @@ def tile_ac4kdotscaleop_kernel(tc, a, b_words, b_scales, bias, out):
             w_sb.append(per_group)
 
         masks.make_identity(nc, ident[:])
-        scale_words = b_scales.bitcast(F32)
+        scale_floats = b_scales.bitcast(F32)
         for q in range(4):
             nc.gpsimd.dma_start(
-                out=planes[32 * q : 32 * q + 16, :].bitcast(F32),
-                in_=scale_words[:, 4 * q : 4 * q + 4, :],
+                out=planes[1][32 * q : 32 * q + 16, :].bitcast(F32),
+                in_=scale_floats[:, 4 * q : 4 * q + 4, N // 8 : N // 4],
             )
 
         warm_ps = psum.tile([P, BANK], F32, tag="bank")
@@ -162,7 +169,9 @@ def tile_ac4kdotscaleop_kernel(tc, a, b_words, b_scales, bias, out):
                             lhsT=a_codes[:, j, g, :].bitcast(FP8X4),
                             lhsT_scale=a_scales[:, j, g, :],
                             rhs=w_sb[c][g][:, t * BANK : (t + 1) * BANK].bitcast(FP8X4),
-                            rhs_scale=planes[4 * g : P, n0 + t * BANK : n0 + (t + 1) * BANK],
+                            rhs_scale=planes[n0 // 2048][
+                                4 * g : P, n0 % 2048 + t * BANK : n0 % 2048 + (t + 1) * BANK
+                            ],
                             start=(g == 0),
                             stop=(g == GROUPS - 1),
                         )

@@ -15,48 +15,39 @@ FLOPS = 2 * M * K * N
 
 P = 128
 GROUPS = K // 512
-ROW_TILES = M // P
+ROWS = M // P
 BANK = 512
 CHUNKS = ((0, 2048), (2048, 1024), (3072, 1024))
-WARM = 5
 
 
 def tile_ac4kdotscaleop_kernel(tc, a, b_words, b_scales, bias, out):
     nc = tc.nc
     with ExitStack() as ctx:
-        ctx.enter_context(tc.manual_schedule())
         keep = ctx.enter_context(tc.tile_pool(name="keep", bufs=1))
         psum = ctx.enter_context(tc.psum_pool(name="psum", bufs=8))
 
-        planes = [keep.tile([P, N // 2], U8, align_bytes=64, name="planes%d" % h) for h in range(2)]
+        planes = keep.tile([P, N], U8, align_bytes=64)
         bias_rows = keep.tile([P, BANK], BF16)
-        warm = keep.tile([P, BANK], BF16)
-        grouped = keep.tile([P, ROW_TILES, GROUPS, P * 4], BF16, align_bytes=64)
-        a_codes = keep.tile([P, ROW_TILES, GROUPS, P], U32, align_bytes=64)
-        a_scales = keep.tile([P, ROW_TILES, GROUPS, P], U8, align_bytes=64)
+        a_sb = keep.tile([P, ROWS * K], BF16)
+        grouped = keep.tile([P, GROUPS, ROWS * P * 4], BF16, align_bytes=64)
+        a_codes = keep.tile([P, GROUPS, ROWS * P], U32, align_bytes=64)
+        a_scales = keep.tile([P, GROUPS, ROWS * P], U8, align_bytes=64)
         bias_bc = keep.tile([P, N], F32)
+        ident_bf = keep.tile([P, P], BF16)
         ident = keep.tile([P, P], F32)
 
         nc.vector.memset(bias_rows[:], 0.0)
-        nc.vector.memset(warm[:], 0.0)
-        nc.vector.memset(planes[0][:].bitcast(I32), 0)
-        nc.vector.memset(planes[1][:].bitcast(I32), 0)
+        nc.vector.memset(planes[:].bitcast(I32), 0)
 
-        a_tiles = a.rearrange("(j p) k -> j p k", p=P)
-        a_sb = []
-        for j in range(ROW_TILES):
-            a_j = keep.tile([P, K], BF16, name="a%d" % j)
-            nc.sync.dma_start(out=a_j[:], in_=a_tiles[j])
-            a_sb.append(a_j)
-            if j == 0:
-                nc.sync.dma_start(
-                    out=bias_rows[0 : N // BANK, :], in_=bias.rearrange("(r n) -> r n", n=BANK)
-                )
+        nc.sync.dma_start(out=a_sb[:], in_=a.rearrange("(p j) k -> p (j k)", j=ROWS))
+        nc.scalar.dma_start(
+            out=bias_rows[0 : N // BANK, :], in_=bias.rearrange("(r n) -> r n", n=BANK)
+        )
         scale_words = b_scales.bitcast(I32)
         for q in range(4):
             nc.sync.dma_start(
-                out=planes[0][32 * q : 32 * q + 16, :].bitcast(I32),
-                in_=scale_words[:, 4 * q : 4 * q + 4, 0 : N // 8],
+                out=planes[32 * q : 32 * q + 16, :].bitcast(I32),
+                in_=scale_words[:, 4 * q : 4 * q + 4, :],
             )
         w_sb = []
         for c, (n0, width) in enumerate(CHUNKS):
@@ -72,86 +63,67 @@ def tile_ac4kdotscaleop_kernel(tc, a, b_words, b_scales, bias, out):
                 per_group.append(w_tile)
             w_sb.append(per_group)
 
+        masks.make_identity(nc, ident_bf[:])
         masks.make_identity(nc, ident[:])
-        scale_floats = b_scales.bitcast(F32)
-        for q in range(4):
-            nc.gpsimd.dma_start(
-                out=planes[1][32 * q : 32 * q + 16, :].bitcast(F32),
-                in_=scale_floats[:, 4 * q : 4 * q + 4, N // 8 : N // 4],
-            )
 
-        warm_ps = psum.tile([P, BANK], F32, tag="bank")
-        for i in range(WARM):
-            nc.tensor.matmul(out=warm_ps[:], lhsT=warm[:, 0:P], rhs=warm[:], start=True, stop=True)
-
-        selector = ident[:].bitcast(BF16)
-
-        def spread_bias(r):
+        def spread_bias(r, engine_copy):
             bank = psum.tile([P, BANK], F32, tag="bank", name="bias_ps%d" % r)
             nc.tensor.matmul(
                 out=bank[:],
-                lhsT=selector[:, 2 * r + 1 : 2 * r + 2].to_broadcast([P, P]),
+                lhsT=ident_bf[:, r : r + 1].to_broadcast([P, P]),
                 rhs=bias_rows[:],
                 start=True,
                 stop=True,
             )
-            return bank
-
-        def keep_bias(r, bank, engine_copy):
             engine_copy(out=bias_bc[:, r * BANK : (r + 1) * BANK], in_=bank[:])
 
-        def transpose_pair(j, pair):
-            a_words = a_sb[j][:].bitcast(F32)
-            xt = psum.tile([P, 2, 2, P], F32, tag="bank", name="xt%d_%d" % (j, pair))
-            for h in range(2):
-                g = 2 * pair + h
+        spread_bias(0, nc.scalar.copy)
+        spread_bias(1, nc.vector.tensor_copy)
+        spread_bias(2, nc.scalar.copy)
+        spread_bias(3, nc.vector.tensor_copy)
+
+        a_words = a_sb[:].bitcast(F32)
+        half = K // 2
+        banks = []
+        for g in range(GROUPS):
+            xt = psum.tile([P, ROWS, 2, P], F32, tag="bank", name="xt%d" % g)
+            for j in range(ROWS):
                 for u in range(2):
                     nc.tensor.transpose(
-                        xt[:, h, u, :], a_words[:, 256 * g + u : 256 * (g + 1) : 2], ident[:]
+                        xt[:, j, u, :],
+                        a_words[:, j * half + 256 * g + u : j * half + 256 * (g + 1) : 2],
+                        ident[:],
                     )
-            return xt
+            banks.append(xt)
 
-        def regroup(j, pair, xt, engine_copy):
+        def regroup(g, engine_copy):
             engine_copy(
-                out=grouped[:, j, 2 * pair : 2 * pair + 2, :]
-                .bitcast(F32)
-                .rearrange("p h (m u) -> p h m u", u=2),
-                in_=xt[:].rearrange("p h u m -> p h m u"),
+                out=grouped[:, g, :].bitcast(F32).rearrange("p (j m u) -> p j m u", j=ROWS, u=2),
+                in_=banks[g][:].rearrange("p j u m -> p j m u"),
             )
 
-        def quantise(j, pair):
+        def quantise(g):
             nc.vector.quantize_mx(
-                out=a_codes[:, j, 2 * pair : 2 * pair + 2, :]
-                .rearrange("p h m -> p (h m)")
-                .bitcast(FP8X4),
-                scales=a_scales[:, j, 2 * pair : 2 * pair + 2, :].rearrange("p h m -> p (h m)"),
-                in_=grouped[:, j, 2 * pair : 2 * pair + 2, :].rearrange("p h c -> p (h c)"),
+                out=a_codes[:, g, :].bitcast(FP8X4),
+                scales=a_scales[:, g, :],
+                in_=grouped[:, g, :],
             )
 
-        xt00 = transpose_pair(0, 0)
-        xt01 = transpose_pair(0, 1)
-        regroup(0, 0, xt00, nc.vector.tensor_copy)
-        regroup(0, 1, xt01, nc.scalar.copy)
-        quantise(0, 0)
-        quantise(0, 1)
-        first = [spread_bias(r) for r in range(4)]
-        keep_bias(0, first[0], nc.scalar.copy)
-        keep_bias(1, first[1], nc.vector.tensor_copy)
-        keep_bias(2, first[2], nc.scalar.copy)
-        keep_bias(3, first[3], nc.vector.tensor_copy)
-        xt10 = transpose_pair(1, 0)
-        xt11 = transpose_pair(1, 1)
-        regroup(1, 0, xt10, nc.vector.tensor_copy)
-        regroup(1, 1, xt11, nc.scalar.copy)
-        quantise(1, 0)
-        quantise(1, 1)
-        second = [spread_bias(r) for r in range(4, 8)]
-        keep_bias(4, second[0], nc.scalar.copy)
-        keep_bias(5, second[1], nc.scalar.copy)
-        keep_bias(6, second[2], nc.vector.tensor_copy)
-        keep_bias(7, second[3], nc.vector.tensor_copy)
+        regroup(0, nc.vector.tensor_copy)
+        regroup(1, nc.scalar.copy)
+        quantise(0)
+        regroup(2, nc.vector.tensor_copy)
+        regroup(3, nc.scalar.copy)
+        quantise(1)
+        quantise(2)
+        quantise(3)
 
-        out_tiles = out.rearrange("(j p) n -> j p n", p=P)
+        spread_bias(4, nc.scalar.copy)
+        spread_bias(5, nc.scalar.copy)
+        spread_bias(6, nc.vector.tensor_copy)
+        spread_bias(7, nc.vector.tensor_copy)
+
+        out_rows = out.rearrange("(p j) n -> p j n", j=ROWS)
         for c, (n0, width) in enumerate(CHUNKS):
             tiles = width // BANK
             acc = [
@@ -159,29 +131,27 @@ def tile_ac4kdotscaleop_kernel(tc, a, b_words, b_scales, bias, out):
                     psum.tile([P, BANK], F32, tag="bank", name="acc%d_%d_%d" % (c, j, t))
                     for t in range(tiles)
                 ]
-                for j in range(ROW_TILES)
+                for j in range(ROWS)
             ]
             for g in range(GROUPS):
-                for j in range(ROW_TILES):
+                for j in range(ROWS):
                     for t in range(tiles):
                         nc.tensor.matmul_mx(
                             out=acc[j][t][:],
-                            lhsT=a_codes[:, j, g, :].bitcast(FP8X4),
-                            lhsT_scale=a_scales[:, j, g, :],
+                            lhsT=a_codes[:, g, j * P : (j + 1) * P].bitcast(FP8X4),
+                            lhsT_scale=a_scales[:, g, j * P : (j + 1) * P],
                             rhs=w_sb[c][g][:, t * BANK : (t + 1) * BANK].bitcast(FP8X4),
-                            rhs_scale=planes[n0 // 2048][
-                                4 * g : P, n0 % 2048 + t * BANK : n0 % 2048 + (t + 1) * BANK
-                            ],
+                            rhs_scale=planes[4 * g : P, n0 + t * BANK : n0 + (t + 1) * BANK],
                             start=(g == 0),
                             stop=(g == GROUPS - 1),
                         )
-            for j in range(ROW_TILES):
-                o_sb = keep.tile([P, width], F32, name="o%d_%d" % (c, j))
+            o_sb = keep.tile([P, ROWS, width], F32, name="o%d" % c)
+            for j in range(ROWS):
                 for t in range(tiles):
                     nc.vector.tensor_tensor(
-                        out=o_sb[:, t * BANK : (t + 1) * BANK],
+                        out=o_sb[:, j, t * BANK : (t + 1) * BANK],
                         in0=acc[j][t][:],
                         in1=bias_bc[:, n0 + t * BANK : n0 + (t + 1) * BANK],
                         op=mybir.AluOpType.add,
                     )
-                nc.sync.dma_start(out=out_tiles[j][:, n0 : n0 + width], in_=o_sb[:])
+            nc.sync.dma_start(out=out_rows[:, :, n0 : n0 + width], in_=o_sb[:])

from contextlib import ExitStack

import concourse.masks as masks
import concourse.mybir as mybir

F32 = mybir.dt.float32
BF16 = mybir.dt.bfloat16
I32 = mybir.dt.int32
U32 = mybir.dt.uint32
U8 = mybir.dt.uint8
FP8X4 = mybir.dt.float8_e4m3fn_x4

M, K, N = 256, 2048, 4096
FLOPS = 2 * M * K * N

P = 128
GROUPS = K // 512
ROWS = M // P
BANK = 512
CHUNKS = ((0, 2048), (2048, 1024), (3072, 1024))


def tile_ac4kdotscaleop_kernel(tc, a, b_words, b_scales, bias, out):
    nc = tc.nc
    with ExitStack() as ctx:
        keep = ctx.enter_context(tc.tile_pool(name="keep", bufs=1))
        psum = ctx.enter_context(tc.psum_pool(name="psum", bufs=8))

        planes = keep.tile([P, N], U8, align_bytes=64)
        bias_rows = keep.tile([P, BANK], BF16)
        a_sb = keep.tile([P, ROWS * K], BF16)
        grouped = keep.tile([P, GROUPS, ROWS * P * 4], BF16, align_bytes=64)
        a_codes = keep.tile([P, GROUPS, ROWS * P], U32, align_bytes=64)
        a_scales = keep.tile([P, GROUPS, ROWS * P], U8, align_bytes=64)
        bias_bc = keep.tile([P, N], F32)
        ident_bf = keep.tile([P, P], BF16)
        ident = keep.tile([P, P], F32)

        nc.vector.memset(bias_rows[:], 0.0)
        nc.vector.memset(planes[:].bitcast(I32), 0)

        nc.sync.dma_start(out=a_sb[:], in_=a.rearrange("(p j) k -> p (j k)", j=ROWS))
        nc.scalar.dma_start(
            out=bias_rows[0 : N // BANK, :], in_=bias.rearrange("(r n) -> r n", n=BANK)
        )
        scale_words = b_scales.bitcast(I32)
        for q in range(4):
            nc.sync.dma_start(
                out=planes[32 * q : 32 * q + 16, :].bitcast(I32),
                in_=scale_words[:, 4 * q : 4 * q + 4, :],
            )
        w_sb = []
        for c, (n0, width) in enumerate(CHUNKS):
            per_group = []
            for g in range(GROUPS):
                w_tile = keep.tile([P, width], U32, align_bytes=64, name="w%d_%d" % (c, g))
                nc.sync.dma_start(
                    out=w_tile[:].bitcast(I32),
                    in_=b_words[g]
                    .rearrange("p n t -> p (n t)")[:, 4 * n0 : 4 * (n0 + width)]
                    .bitcast(I32),
                )
                per_group.append(w_tile)
            w_sb.append(per_group)

        masks.make_identity(nc, ident_bf[:])
        masks.make_identity(nc, ident[:])

        def spread_bias(r, engine_copy):
            bank = psum.tile([P, BANK], F32, tag="bank", name="bias_ps%d" % r)
            nc.tensor.matmul(
                out=bank[:],
                lhsT=ident_bf[:, r : r + 1].to_broadcast([P, P]),
                rhs=bias_rows[:],
                start=True,
                stop=True,
            )
            engine_copy(out=bias_bc[:, r * BANK : (r + 1) * BANK], in_=bank[:])

        spread_bias(0, nc.scalar.copy)
        spread_bias(1, nc.vector.tensor_copy)
        spread_bias(2, nc.scalar.copy)
        spread_bias(3, nc.vector.tensor_copy)

        a_words = a_sb[:].bitcast(F32)
        half = K // 2
        banks = []
        for g in range(GROUPS):
            xt = psum.tile([P, ROWS, 2, P], F32, tag="bank", name="xt%d" % g)
            for j in range(ROWS):
                for u in range(2):
                    nc.tensor.transpose(
                        xt[:, j, u, :],
                        a_words[:, j * half + 256 * g + u : j * half + 256 * (g + 1) : 2],
                        ident[:],
                    )
            banks.append(xt)

        def regroup(g, engine_copy):
            engine_copy(
                out=grouped[:, g, :].bitcast(F32).rearrange("p (j m u) -> p j m u", j=ROWS, u=2),
                in_=banks[g][:].rearrange("p j u m -> p j m u"),
            )

        def quantise(g):
            nc.vector.quantize_mx(
                out=a_codes[:, g, :].bitcast(FP8X4),
                scales=a_scales[:, g, :],
                in_=grouped[:, g, :],
            )

        regroup(0, nc.vector.tensor_copy)
        regroup(1, nc.scalar.copy)
        quantise(0)
        regroup(2, nc.vector.tensor_copy)
        regroup(3, nc.scalar.copy)
        quantise(1)
        quantise(2)
        quantise(3)

        spread_bias(4, nc.scalar.copy)
        spread_bias(5, nc.scalar.copy)
        spread_bias(6, nc.vector.tensor_copy)
        spread_bias(7, nc.vector.tensor_copy)

        out_rows = out.rearrange("(p j) n -> p j n", j=ROWS)
        for c, (n0, width) in enumerate(CHUNKS):
            tiles = width // BANK
            acc = [
                [
                    psum.tile([P, BANK], F32, tag="bank", name="acc%d_%d_%d" % (c, j, t))
                    for t in range(tiles)
                ]
                for j in range(ROWS)
            ]
            for g in range(GROUPS):
                for j in range(ROWS):
                    for t in range(tiles):
                        nc.tensor.matmul_mx(
                            out=acc[j][t][:],
                            lhsT=a_codes[:, g, j * P : (j + 1) * P].bitcast(FP8X4),
                            lhsT_scale=a_scales[:, g, j * P : (j + 1) * P],
                            rhs=w_sb[c][g][:, t * BANK : (t + 1) * BANK].bitcast(FP8X4),
                            rhs_scale=planes[4 * g : P, n0 + t * BANK : n0 + (t + 1) * BANK],
                            start=(g == 0),
                            stop=(g == GROUPS - 1),
                        )
            o_sb = keep.tile([P, ROWS, width], F32, name="o%d" % c)
            for j in range(ROWS):
                for t in range(tiles):
                    nc.vector.tensor_tensor(
                        out=o_sb[:, j, t * BANK : (t + 1) * BANK],
                        in0=acc[j][t][:],
                        in1=bias_bc[:, n0 + t * BANK : n0 + (t + 1) * BANK],
                        op=mybir.AluOpType.add,
                    )
            nc.sync.dma_start(out=out_rows[:, :, n0 : n0 + width], in_=o_sb[:])
